import numpy as np
import ml_dtypes


def mxq(x, axis, fmt="e4m3"):
    dtype, down = {"e4m3": (ml_dtypes.float8_e4m3fn, 7), "e5m2": (ml_dtypes.float8_e5m2, 14)}[fmt]
    v = np.moveaxis(np.asarray(x, np.float32).astype(ml_dtypes.bfloat16).astype(np.float64), axis, -1)
    blocks = v.reshape(v.shape[:-1] + (-1, 32))
    amax = np.abs(blocks).max(-1, keepdims=True)
    byte = np.maximum(np.where(amax > 0, np.frexp(amax)[1] - 1 + 127, 0) - down, 1)
    scale = np.exp2(byte - 127.0)
    codes = (blocks / scale).astype(np.float32).astype(dtype).astype(np.float64)
    return np.moveaxis((codes * scale).reshape(v.shape), -1, axis)


WIDE = False


def mx_kscale(k):
    if not WIDE:
        return np.ones(k)
    levels = np.array([10, -10, 5, -5, 0])
    a = np.random.permutation(np.resize(levels, k // 512 * 4)).reshape(k // 512, 4)
    idx = np.arange(k)
    return np.exp2(a[idx // 512, idx % 128 // 32])


BF16 = ml_dtypes.bfloat16


def bf(x):
    return np.asarray(x, np.float32).astype(BF16)


def f64(x):
    return np.asarray(x).astype(np.float64)


E2M1 = np.array([0.0, 0.5, 1.0, 1.5, 2.0, 3.0, 4.0, 6.0, -0.0, -0.5, -1.0, -1.5, -2.0, -3.0, -4.0, -6.0])


def pack_weight(w, fmt):
    k, n = w.shape
    w = f64(bf(w)).reshape(k // 32, 32, n)
    amax = np.abs(w).max(1)
    if fmt == "e4m3":
        byte = np.frexp(amax)[1] - 1 + 127 - 7
    else:
        mant, ex = np.frexp(amax / 6.0)
        byte = np.where(mant > 0.5, ex, ex - 1) + 127
    byte = np.clip(np.where(amax > 0, byte, 1), 1, 254)
    scaled = (w * np.exp2(127.0 - byte)[:, None, :]).reshape(k, n).astype(np.float32)
    by_word = np.ascontiguousarray(scaled.reshape(k // 512, 128, 4, n).transpose(0, 1, 3, 2))
    if fmt == "e4m3":
        words = by_word.astype(ml_dtypes.float8_e4m3fn).view(np.uint8)
    else:
        c = by_word.astype(ml_dtypes.float4_e2m1fn).view(np.uint8) & 0xF
        words = c[..., 0::2] | (c[..., 1::2] << 4)
    return np.ascontiguousarray(words), np.ascontiguousarray(byte.astype(np.uint8).reshape(k // 512, 16, n))


def unpack_weight(words, scales, fmt):
    g, p, n, _ = words.shape
    if fmt == "e4m3":
        vals = np.ascontiguousarray(words).view(ml_dtypes.float8_e4m3fn).astype(np.float64)
    else:
        nib = np.empty((g, p, n, 4), np.uint8)
        nib[..., 0::2] = words & 0xF
        nib[..., 1::2] = words >> 4
        vals = E2M1[nib]
    vals = vals * np.repeat(np.exp2(scales.astype(np.float64) - 127.0), 8, axis=1)[..., None]
    return vals.transpose(0, 1, 3, 2).reshape(g * 512, n)


B, T, N, C = 4, 4, 512, 512
EDGE = 0.0625


def sigmoid(z):
    return 1.0 / (1.0 + np.exp(-z))


def setup_inputs():
    s = mx_kscale(C)
    x = bf(np.random.standard_normal((B, T, N, C)) * 0.5)
    hid = bf(np.maximum(np.random.standard_normal((B, T, N, C)), 0.0) * s)
    adj = bf(np.random.random((B, N, N)) * (np.random.random((B, N, N)) < EDGE))
    lam_raw = bf(3.5 + 0.1 * np.random.standard_normal(1))
    words, scales = pack_weight(np.random.standard_normal((C, C)) * 4.5 / np.sqrt(C) / s[:, None], "e4m3")
    return {"x": x,
            "hid": hid,
            "adj": adj,
            "lam_raw": lam_raw,
            "theta_words": words,
            "theta_scales": scales}


def reference(x, hid, adj, lam_raw, theta_words, theta_scales):
    lam = 1.0 + np.maximum(f64(lam_raw)[0], 0.0)
    h = mxq(f64(hid), 3, "e4m3") @ unpack_weight(theta_words, theta_scales, "e4m3")
    v = ((2.0 * lam - 2.0) / lam) * np.eye(N) + (2.0 / lam) * f64(adj)
    v = v / np.sum(v, axis=-1, keepdims=True)
    out = mxq(v, 2, "e4m3")[:, None] @ mxq(h, 2, "e4m3")
    return np.maximum(f64(x), 0.0) + sigmoid(np.maximum(out, 0.0))

@@ -1,0 +1,257 @@
+from contextlib import ExitStack
+
+import concourse.mybir as mybir
+from concourse.masks import make_identity
+
+F32 = mybir.dt.float32
+BF16 = mybir.dt.bfloat16
+I32 = mybir.dt.int32
+U32 = mybir.dt.uint32
+U8 = mybir.dt.uint8
+FP8X4 = mybir.dt.float8_e4m3fn_x4
+ALU = mybir.AluOpType
+ACT = mybir.ActivationFunctionType
+
+P = 128
+PACK = 4
+B, T, N, C = 4, 4, 512, 512
+UNITS = B * T
+PARTS = B * PACK
+FLOPS = 2 * B * T * N * C * C + 2 * B * T * N * N * C
+
+
+def cols(k):
+    return slice(k * P, (k + 1) * P)
+
+
+def tile_akgcn_pb_t_kernel(tc, x, hid, adj, lam_raw, theta_words, theta_scales, out):
+    nc = tc.nc
+    hid_units = hid.rearrange("b t (p j) c -> (b t) p j c", j=PACK)
+    x_units = x.rearrange("b t (p i) c -> (b t) p i c", i=PACK)
+    out_units = out.rearrange("b t (p i) c -> (b t) p i c", i=PACK)
+    adj_rows = adj.rearrange("b (p i) m -> b p i m", i=PACK)
+
+    with ExitStack() as stack:
+        consts = stack.enter_context(tc.tile_pool(name="consts", bufs=1))
+        loads = stack.enter_context(tc.tile_pool(name="loads", bufs=4))
+        work = stack.enter_context(tc.tile_pool(name="work", bufs=2))
+        small = stack.enter_context(tc.tile_pool(name="small", bufs=4))
+        psum_hidT = stack.enter_context(tc.psum_pool(name="psum_hidT", bufs=2))
+        psum_vT = stack.enter_context(tc.psum_pool(name="psum_vT", bufs=1))
+        psum_h = stack.enter_context(tc.psum_pool(name="psum_h", bufs=3))
+        psum_g = stack.enter_context(tc.psum_pool(name="psum_g", bufs=2))
+
+        lam_bf = consts.tile([P, 1], BF16)
+        nc.sync.dma_start(out=lam_bf[:], in_=lam_raw.partition_broadcast(P))
+
+        theta_plane = consts.tile([P, C], U8, align_bytes=64)
+        nc.vector.memset(theta_plane[:].bitcast(I32), 0)
+        for quadrant in range(4):
+            nc.sync.dma_start(
+                out=theta_plane[32 * quadrant : 32 * quadrant + 4, :].bitcast(I32),
+                in_=theta_scales[0, 4 * quadrant : 4 * quadrant + 4, :].bitcast(I32),
+            )
+        theta_codes = consts.tile([P, C], U32, align_bytes=64)
+        nc.sync.dma_start(
+            out=theta_codes[:].bitcast(I32),
+            in_=theta_words[0].rearrange("p n t -> p (n t)").bitcast(I32),
+        )
+
+        ident_f32 = consts.tile([P, P], F32)
+        make_identity(nc, ident_f32[:])
+        ident_bf = consts.tile([P, P], BF16)
+        make_identity(nc, ident_bf[:])
+
+        w = consts.tile([P, 1], F32)
+        nc.vector.tensor_scalar_max(out=w[:], in0=lam_bf[:], scalar1=0.0)
+        w_diag = consts.tile([P, PACK, N], BF16)
+        nc.vector.memset(w_diag[:], 0.0)
+        for i in range(PACK):
+            nc.vector.tensor_scalar(
+                out=w_diag[:, i, :].rearrange("p (q t) -> p q t", t=PACK)[:, :, i],
+                in0=ident_bf[:],
+                scalar1=w[:, 0:1],
+                scalar2=None,
+                op0=ALU.mult,
+            )
+
+        vT_codes = consts.tile([P, PARTS, P], U32, align_bytes=64)
+        vT_plane = consts.tile([P, PARTS, P], U8, align_bytes=64)
+
+        adj_sb, hid_sb, x_sb, out_sb = {}, {}, {}, {}
+        v_rows, vT_ps, vT_grouped = {}, {}, {}
+        hidT_grouped, hid_codes, hid_plane = {}, {}, {}
+        h_grouped, h_codes, h_plane = {}, {}, {}
+
+        def load_adj(part):
+            if 0 <= part < PARTS and part % PACK == 0:
+                b = part // PACK
+                adj_sb[b] = loads.tile([P, PACK, N], BF16, name="adj_sb", bufs=2)
+                nc.sync.dma_start(out=adj_sb[b][:], in_=adj_rows[b])
+
+        def load_hid(u):
+            if 0 <= u < UNITS:
+                hid_sb[u] = loads.tile([P, PACK, C], BF16, name="hid_sb")
+                nc.sync.dma_start(out=hid_sb[u][:], in_=hid_units[u])
+
+        def load_x(u):
+            if 0 <= u < UNITS:
+                x_sb[u] = loads.tile([P, PACK, C], BF16, name="x_sb", bufs=5)
+                nc.sync.dma_start(out=x_sb[u][:], in_=x_units[u])
+
+        def normalise_v(part):
+            if not 0 <= part < PARTS:
+                return
+            b, i = divmod(part, PACK)
+            with_diag = work.tile([P, N], F32, name="with_diag")
+            row_sum = small.tile([P, 1], F32, name="row_sum")
+            nc.vector.scalar_tensor_tensor(
+                out=with_diag[:],
+                in0=adj_sb[b][:, i, :],
+                scalar=1.0,
+                in1=w_diag[:, i, :],
+                op0=ALU.mult,
+                op1=ALU.add,
+                accum_out=row_sum[:],
+            )
+            inv_sum = small.tile([P, 1], F32, name="inv_sum")
+            nc.vector.reciprocal(out=inv_sum[:], in_=row_sum[:])
+            v_rows[part] = work.tile([P, N], BF16, name="v_rows")
+            nc.vector.tensor_scalar(
+                out=v_rows[part][:], in0=with_diag[:], scalar1=inv_sum[:, 0:1], scalar2=None, op0=ALU.mult
+            )
+
+        def transpose_v(part):
+            if not 0 <= part < PARTS:
+                return
+            vT_ps[part] = psum_vT.tile([P, PACK, P], BF16, name="vT_ps")
+            for t in range(PACK):
+                nc.tensor.transpose(vT_ps[part][:, t, :], v_rows[part][:, t:N:PACK], ident_bf[:])
+
+        def group_v(part):
+            if not 0 <= part < PARTS:
+                return
+            vT_grouped[part] = work.tile([P, P, PACK], BF16, name="vT_grouped", align_bytes=64)
+            nc.vector.tensor_copy(out=vT_grouped[part][:], in_=vT_ps[part][:].rearrange("q t p -> q p t"))
+
+        def quantise_v(part):
+            if not 0 <= part < PARTS:
+                return
+            nc.vector.quantize_mx(
+                out=vT_codes[:, part, :].bitcast(FP8X4),
+                scales=vT_plane[:, part, :],
+                in_=vT_grouped[part][:].rearrange("q p t -> q (p t)"),
+            )
+
+        def transpose_hid(u):
+            if not 0 <= u < UNITS:
+                return
+            hid_words = hid_sb[u][:].bitcast(F32)
+            hidT_grouped[u] = work.tile([P, PACK, P, PACK], BF16, name="hidT_grouped", align_bytes=64)
+            grouped_words = hidT_grouped[u][:].bitcast(F32)
+            for half in range(2):
+                hidT_ps = psum_hidT.tile([P, 2, 2, P], F32, name="hidT_ps")
+                for jj in range(2):
+                    for pair in range(2):
+                        nc.tensor.transpose(
+                            hidT_ps[:, jj, pair, :],
+                            hid_words[:, 2 * half + jj, pair : C // 2 : 2],
+                            ident_f32[:],
+                        )
+                nc.scalar.copy(
+                    out=grouped_words[:, 2 * half : 2 * half + 2, :, :],
+                    in_=hidT_ps[:].rearrange("q jj pair p -> q jj p pair"),
+                )
+
+        def quantise_hid(u):
+            if not 0 <= u < UNITS:
+                return
+            hid_codes[u] = work.tile([P, N], U32, name="hid_codes", align_bytes=64)
+            hid_plane[u] = work.tile([P, N], U8, name="hid_plane", align_bytes=64)
+            nc.vector.quantize_mx(
+                out=hid_codes[u][:].bitcast(FP8X4),
+                scales=hid_plane[u][:],
+                in_=hidT_grouped[u][:].rearrange("q j p t -> q (j p t)"),
+            )
+
+        def first_matmul(u):
+            if not 0 <= u < UNITS:
+                return
+            h_grouped[u] = work.tile([P, C, PACK], BF16, name="h_grouped", align_bytes=64)
+            for cb in range(C // P):
+                h_ps = psum_h.tile([P, PACK, P], F32, name="h_ps")
+                for j in range(PACK):
+                    nc.tensor.matmul_mx(
+                        out=h_ps[:, j, :],
+                        lhsT=hid_codes[u][:, cols(j)].bitcast(FP8X4),
+                        lhsT_scale=hid_plane[u][:, cols(j)],
+                        rhs=theta_codes[:, cols(cb)].bitcast(FP8X4),
+                        rhs_scale=theta_plane[:, cols(cb)],
+                        start=True,
+                        stop=True,
+                    )
+                nc.scalar.copy(out=h_grouped[u][:, cols(cb), :], in_=h_ps[:].rearrange("p j c -> p c j"))
+
+        def quantise_h(u):
+            if not 0 <= u < UNITS:
+                return
+            h_codes[u] = work.tile([P, C], U32, name="h_codes", align_bytes=64)
+            h_plane[u] = work.tile([P, C], U8, name="h_plane", align_bytes=64)
+            nc.vector.quantize_mx(
+                out=h_codes[u][:].bitcast(FP8X4),
+                scales=h_plane[u][:],
+                in_=h_grouped[u][:].rearrange("p c j -> p (c j)"),
+            )
+
+        def second_matmul(u):
+            if not 0 <= u < UNITS:
+                return
+            b = u // T
+            out_sb[u] = loads.tile([P, PACK, C], F32, name="out_sb")
+            for i in range(PACK):
+                g_ps = psum_g.tile([P, C], F32, name="g_ps")
+                nc.tensor.matmul_mx(
+                    out=g_ps[:],
+                    lhsT=vT_codes[:, b * PACK + i, :].bitcast(FP8X4),
+                    lhsT_scale=vT_plane[:, b * PACK + i, :],
+                    rhs=h_codes[u][:].bitcast(FP8X4),
+                    rhs_scale=h_plane[u][:],
+                    start=True,
+                    stop=True,
+                )
+                nc.scalar.activation(out=out_sb[u][:, i, :], in_=g_ps[:], func=ACT.Sigmoid)
+
+        def relu_x(u):
+            if not 0 <= u < UNITS:
+                return
+            nc.vector.tensor_scalar_max(out=x_sb[u][:], in0=x_sb[u][:], scalar1=0.0)
+
+        def finish(u):
+            if not 0 <= u < UNITS:
+                return
+            flat = out_sb[u][:].rearrange("p i c -> p (i c)")
+            nc.vector.scalar_tensor_tensor(
+                out=flat,
+                in0=flat,
+                scalar=0.5,
+                in1=x_sb[u][:].rearrange("p i c -> p (i c)"),
+                op0=ALU.max,
+                op1=ALU.add,
+            )
+            nc.sync.dma_start(out=out_units[u], in_=out_sb[u][:])
+
+        for step in range(-7, UNITS + 1):
+            load_adj(step + 7)
+            load_hid(step + 4)
+            load_x(step + 3)
+            finish(step - 1)
+            transpose_hid(step + 2)
+            transpose_v(step + 4)
+            normalise_v(step + 5)
+            quantise_hid(step + 2)
+            first_matmul(step + 1)
+            relu_x(step)
+            group_v(step + 4)
+            quantise_h(step + 1)
+            quantise_v(step + 4)
+            second_matmul(step)

@@ -41,8 +41,33 @@ def tile_akgcn_pb_t_kernel(tc, x, hid, adj, lam_raw, theta_words, theta_scales, 
         psum_h = stack.enter_context(tc.psum_pool(name="psum_h", bufs=3))
         psum_g = stack.enter_context(tc.psum_pool(name="psum_g", bufs=2))
 
+        stack.enter_context(tc.manual_schedule())
+
+        adj_sb, hid_sb, x_sb, out_sb = {}, {}, {}, {}
+        with_diag, row_sum, inv_sum, v_rows, vT_ps, vT_grouped = {}, {}, {}, {}, {}, {}
+        hidT_grouped, hid_codes, hid_plane = {}, {}, {}
+        h_grouped, h_codes, h_plane = {}, {}, {}
+
+        def load_adj(part):
+            b = part // PACK
+            if 0 <= part < PARTS and b not in adj_sb:
+                adj_sb[b] = loads.tile([P, PACK, N], BF16, name="adj_sb", bufs=2)
+                nc.sync.dma_start(out=adj_sb[b][:], in_=adj_rows[b])
+
+        def load_hid(u):
+            if 0 <= u < UNITS and u not in hid_sb:
+                hid_sb[u] = loads.tile([P, PACK, C], BF16, name="hid_sb")
+                nc.sync.dma_start(out=hid_sb[u][:], in_=hid_units[u])
+
+        def load_x(u):
+            if 0 <= u < UNITS:
+                x_sb[u] = loads.tile([P, PACK, C], BF16, name="x_sb", bufs=5)
+                nc.sync.dma_start(out=x_sb[u][:], in_=x_units[u])
+
         lam_bf = consts.tile([P, 1], BF16)
         nc.sync.dma_start(out=lam_bf[:], in_=lam_raw.partition_broadcast(P))
+        load_hid(0)
+        load_adj(0)
 
         theta_plane = consts.tile([P, C], U8, align_bytes=64)
         nc.vector.memset(theta_plane[:].bitcast(I32), 0)
@@ -78,47 +103,38 @@ def tile_akgcn_pb_t_kernel(tc, x, hid, adj, lam_raw, theta_words, theta_scales, 
         vT_codes = consts.tile([P, PARTS, P], U32, align_bytes=64)
         vT_plane = consts.tile([P, PARTS, P], U8, align_bytes=64)
 
-        adj_sb, hid_sb, x_sb, out_sb = {}, {}, {}, {}
-        v_rows, vT_ps, vT_grouped = {}, {}, {}
-        hidT_grouped, hid_codes, hid_plane = {}, {}, {}
-        h_grouped, h_codes, h_plane = {}, {}, {}
-
-        def load_adj(part):
-            if 0 <= part < PARTS and part % PACK == 0:
-                b = part // PACK
-                adj_sb[b] = loads.tile([P, PACK, N], BF16, name="adj_sb", bufs=2)
-                nc.sync.dma_start(out=adj_sb[b][:], in_=adj_rows[b])
-
-        def load_hid(u):
-            if 0 <= u < UNITS:
-                hid_sb[u] = loads.tile([P, PACK, C], BF16, name="hid_sb")
-                nc.sync.dma_start(out=hid_sb[u][:], in_=hid_units[u])
-
-        def load_x(u):
-            if 0 <= u < UNITS:
-                x_sb[u] = loads.tile([P, PACK, C], BF16, name="x_sb", bufs=5)
-                nc.sync.dma_start(out=x_sb[u][:], in_=x_units[u])
-
-        def normalise_v(part):
+        def sum_v_rows(part):
             if not 0 <= part < PARTS:
                 return
             b, i = divmod(part, PACK)
-            with_diag = work.tile([P, N], F32, name="with_diag")
-            row_sum = small.tile([P, 1], F32, name="row_sum")
+            with_diag[part] = work.tile([P, N], F32, name="with_diag")
+            row_sum[part] = small.tile([P, 1], F32, name="row_sum")
             nc.vector.scalar_tensor_tensor(
-                out=with_diag[:],
+                out=with_diag[part][:],
                 in0=adj_sb[b][:, i, :],
                 scalar=1.0,
                 in1=w_diag[:, i, :],
                 op0=ALU.mult,
                 op1=ALU.add,
-                accum_out=row_sum[:],
+                accum_out=row_sum[part][:],
             )
-            inv_sum = small.tile([P, 1], F32, name="inv_sum")
-            nc.vector.reciprocal(out=inv_sum[:], in_=row_sum[:])
+
+        def invert_v_sums(part):
+            if not 0 <= part < PARTS:
+                return
+            inv_sum[part] = small.tile([P, 1], F32, name="inv_sum")
+            nc.vector.reciprocal(out=inv_sum[part][:], in_=row_sum[part][:])
+
+        def scale_v_rows(part):
+            if not 0 <= part < PARTS:
+                return
             v_rows[part] = work.tile([P, N], BF16, name="v_rows")
             nc.vector.tensor_scalar(
-                out=v_rows[part][:], in0=with_diag[:], scalar1=inv_sum[:, 0:1], scalar2=None, op0=ALU.mult
+                out=v_rows[part][:],
+                in0=with_diag[part][:],
+                scalar1=inv_sum[part][:, 0:1],
+                scalar2=None,
+                op0=ALU.mult,
             )
 
         def transpose_v(part):
@@ -143,25 +159,25 @@ def tile_akgcn_pb_t_kernel(tc, x, hid, adj, lam_raw, theta_words, theta_scales, 
                 in_=vT_grouped[part][:].rearrange("q p t -> q (p t)"),
             )
 
-        def transpose_hid(u):
+        def transpose_hid(u, half):
             if not 0 <= u < UNITS:
                 return
+            if half == 0:
+                hidT_grouped[u] = work.tile([P, PACK, P, PACK], BF16, name="hidT_grouped", align_bytes=64)
             hid_words = hid_sb[u][:].bitcast(F32)
-            hidT_grouped[u] = work.tile([P, PACK, P, PACK], BF16, name="hidT_grouped", align_bytes=64)
             grouped_words = hidT_grouped[u][:].bitcast(F32)
-            for half in range(2):
-                hidT_ps = psum_hidT.tile([P, 2, 2, P], F32, name="hidT_ps")
-                for jj in range(2):
-                    for pair in range(2):
-                        nc.tensor.transpose(
-                            hidT_ps[:, jj, pair, :],
-                            hid_words[:, 2 * half + jj, pair : C // 2 : 2],
-                            ident_f32[:],
-                        )
-                nc.scalar.copy(
-                    out=grouped_words[:, 2 * half : 2 * half + 2, :, :],
-                    in_=hidT_ps[:].rearrange("q jj pair p -> q jj p pair"),
-                )
+            hidT_ps = psum_hidT.tile([P, 2, 2, P], F32, name="hidT_ps")
+            for jj in range(2):
+                for pair in range(2):
+                    nc.tensor.transpose(
+                        hidT_ps[:, jj, pair, :],
+                        hid_words[:, 2 * half + jj, pair : C // 2 : 2],
+                        ident_f32[:],
+                    )
+            nc.scalar.copy(
+                out=grouped_words[:, 2 * half : 2 * half + 2, :, :],
+                in_=hidT_ps[:].rearrange("q jj pair p -> q jj p pair"),
+            )
 
         def quantise_hid(u):
             if not 0 <= u < UNITS:
@@ -174,23 +190,23 @@ def tile_akgcn_pb_t_kernel(tc, x, hid, adj, lam_raw, theta_words, theta_scales, 
                 in_=hidT_grouped[u][:].rearrange("q j p t -> q (j p t)"),
             )
 
-        def first_matmul(u):
+        def first_matmul(u, cb):
             if not 0 <= u < UNITS:
                 return
-            h_grouped[u] = work.tile([P, C, PACK], BF16, name="h_grouped", align_bytes=64)
-            for cb in range(C // P):
-                h_ps = psum_h.tile([P, PACK, P], F32, name="h_ps")
-                for j in range(PACK):
-                    nc.tensor.matmul_mx(
-                        out=h_ps[:, j, :],
-                        lhsT=hid_codes[u][:, cols(j)].bitcast(FP8X4),
-                        lhsT_scale=hid_plane[u][:, cols(j)],
-                        rhs=theta_codes[:, cols(cb)].bitcast(FP8X4),
-                        rhs_scale=theta_plane[:, cols(cb)],
-                        start=True,
-                        stop=True,
-                    )
-                nc.scalar.copy(out=h_grouped[u][:, cols(cb), :], in_=h_ps[:].rearrange("p j c -> p c j"))
+            if cb == 0:
+                h_grouped[u] = work.tile([P, C, PACK], BF16, name="h_grouped", align_bytes=64)
+            h_ps = psum_h.tile([P, PACK, P], F32, name="h_ps")
+            for j in range(PACK):
+                nc.tensor.matmul_mx(
+                    out=h_ps[:, j, :],
+                    lhsT=hid_codes[u][:, cols(j)].bitcast(FP8X4),
+                    lhsT_scale=hid_plane[u][:, cols(j)],
+                    rhs=theta_codes[:, cols(cb)].bitcast(FP8X4),
+                    rhs_scale=theta_plane[:, cols(cb)],
+                    start=True,
+                    stop=True,
+                )
+            nc.scalar.copy(out=h_grouped[u][:, cols(cb), :], in_=h_ps[:].rearrange("p j c -> p c j"))
 
         def quantise_h(u):
             if not 0 <= u < UNITS:
@@ -203,23 +219,23 @@ def tile_akgcn_pb_t_kernel(tc, x, hid, adj, lam_raw, theta_words, theta_scales, 
                 in_=h_grouped[u][:].rearrange("p c j -> p (c j)"),
             )
 
-        def second_matmul(u):
+        def second_matmul(u, i):
             if not 0 <= u < UNITS:
                 return
-            b = u // T
-            out_sb[u] = loads.tile([P, PACK, C], F32, name="out_sb")
-            for i in range(PACK):
-                g_ps = psum_g.tile([P, C], F32, name="g_ps")
-                nc.tensor.matmul_mx(
-                    out=g_ps[:],
-                    lhsT=vT_codes[:, b * PACK + i, :].bitcast(FP8X4),
-                    lhsT_scale=vT_plane[:, b * PACK + i, :],
-                    rhs=h_codes[u][:].bitcast(FP8X4),
-                    rhs_scale=h_plane[u][:],
-                    start=True,
-                    stop=True,
-                )
-                nc.scalar.activation(out=out_sb[u][:, i, :], in_=g_ps[:], func=ACT.Sigmoid)
+            if i == 0:
+                out_sb[u] = loads.tile([P, PACK, C], F32, name="out_sb")
+            part = (u // T) * PACK + i
+            g_ps = psum_g.tile([P, C], F32, name="g_ps")
+            nc.tensor.matmul_mx(
+                out=g_ps[:],
+                lhsT=vT_codes[:, part, :].bitcast(FP8X4),
+                lhsT_scale=vT_plane[:, part, :],
+                rhs=h_codes[u][:].bitcast(FP8X4),
+                rhs_scale=h_plane[u][:],
+                start=True,
+                stop=True,
+            )
+            nc.scalar.activation(out=out_sb[u][:, i, :], in_=g_ps[:], func=ACT.Sigmoid)
 
         def relu_x(u):
             if not 0 <= u < UNITS:
@@ -240,18 +256,24 @@ def tile_akgcn_pb_t_kernel(tc, x, hid, adj, lam_raw, theta_words, theta_scales, 
             )
             nc.sync.dma_start(out=out_units[u], in_=out_sb[u][:])
 
-        for step in range(-7, UNITS + 1):
-            load_adj(step + 7)
-            load_hid(step + 4)
+        for step in range(-6, UNITS + 1):
+            load_adj(step + 8)
+            load_hid(step + 6)
             load_x(step + 3)
+
             finish(step - 1)
-            transpose_hid(step + 2)
-            transpose_v(step + 4)
-            normalise_v(step + 5)
-            quantise_hid(step + 2)
-            first_matmul(step + 1)
-            relu_x(step)
+            sum_v_rows(step + 6)
+            quantise_hid(step + 3)
+            invert_v_sums(step + 6)
             group_v(step + 4)
+            scale_v_rows(step + 6)
             quantise_h(step + 1)
+            relu_x(step)
             quantise_v(step + 4)
-            second_matmul(step)
+
+            for k in range(PACK):
+                first_matmul(step + 2, k)
+                second_matmul(step, k)
+                if k % 2 == 1:
+                    transpose_hid(step + 4, k // 2)
+            transpose_v(step + 5)

@@ -64,9 +64,9 @@ def tile_akgcn_pb_t_kernel(tc, x, hid, adj, lam_raw, theta_words, theta_scales, 
                 x_sb[u] = loads.tile([P, PACK, C], BF16, name="x_sb", bufs=5)
                 nc.sync.dma_start(out=x_sb[u][:], in_=x_units[u])
 
+        load_hid(0)
         lam_bf = consts.tile([P, 1], BF16)
         nc.sync.dma_start(out=lam_bf[:], in_=lam_raw.partition_broadcast(P))
-        load_hid(0)
         load_adj(0)
 
         theta_plane = consts.tile([P, C], U8, align_bytes=64)
@@ -148,7 +148,8 @@ def tile_akgcn_pb_t_kernel(tc, x, hid, adj, lam_raw, theta_words, theta_scales, 
             if not 0 <= part < PARTS:
                 return
             vT_grouped[part] = work.tile([P, P, PACK], BF16, name="vT_grouped", align_bytes=64)
-            nc.vector.tensor_copy(out=vT_grouped[part][:], in_=vT_ps[part][:].rearrange("q t p -> q p t"))
+            copy = nc.scalar.copy if part % 2 == 0 else nc.vector.tensor_copy
+            copy(out=vT_grouped[part][:], in_=vT_ps[part][:].rearrange("q t p -> q p t"))
 
         def quantise_v(part):
             if not 0 <= part < PARTS:
@@ -182,8 +183,8 @@ def tile_akgcn_pb_t_kernel(tc, x, hid, adj, lam_raw, theta_words, theta_scales, 
         def quantise_hid(u):
             if not 0 <= u < UNITS:
                 return
-            hid_codes[u] = work.tile([P, N], U32, name="hid_codes", align_bytes=64)
-            hid_plane[u] = work.tile([P, N], U8, name="hid_plane", align_bytes=64)
+            hid_codes[u] = work.tile([P, N], U32, name="hid_codes", align_bytes=64, bufs=3)
+            hid_plane[u] = work.tile([P, N], U8, name="hid_plane", align_bytes=64, bufs=3)
             nc.vector.quantize_mx(
                 out=hid_codes[u][:].bitcast(FP8X4),
                 scales=hid_plane[u][:],
@@ -245,25 +246,28 @@ def tile_akgcn_pb_t_kernel(tc, x, hid, adj, lam_raw, theta_words, theta_scales, 
         def finish(u):
             if not 0 <= u < UNITS:
                 return
-            flat = out_sb[u][:].rearrange("p i c -> p (i c)")
-            nc.vector.scalar_tensor_tensor(
-                out=flat,
-                in0=flat,
-                scalar=0.5,
-                in1=x_sb[u][:].rearrange("p i c -> p (i c)"),
-                op0=ALU.max,
-                op1=ALU.add,
-            )
-            nc.sync.dma_start(out=out_units[u], in_=out_sb[u][:])
+            groups = 1 if u == UNITS - 1 else PACK
+            for first in range(0, PACK, groups):
+                piece = slice(first, first + groups)
+                flat = out_sb[u][:, piece, :].rearrange("p i c -> p (i c)")
+                nc.vector.scalar_tensor_tensor(
+                    out=flat,
+                    in0=flat,
+                    scalar=0.5,
+                    in1=x_sb[u][:, piece, :].rearrange("p i c -> p (i c)"),
+                    op0=ALU.max,
+                    op1=ALU.add,
+                )
+                nc.sync.dma_start(out=out_units[u][:, piece, :], in_=out_sb[u][:, piece, :])
 
         for step in range(-6, UNITS + 1):
             load_adj(step + 8)
-            load_hid(step + 6)
+            load_hid(step + 7)
             load_x(step + 3)
 
             finish(step - 1)
             sum_v_rows(step + 6)
-            quantise_hid(step + 3)
+            quantise_hid(step + 4)
             invert_v_sums(step + 6)
             group_v(step + 4)
             scale_v_rows(step + 6)
@@ -275,5 +279,5 @@ def tile_akgcn_pb_t_kernel(tc, x, hid, adj, lam_raw, theta_words, theta_scales, 
                 first_matmul(step + 2, k)
                 second_matmul(step, k)
                 if k % 2 == 1:
-                    transpose_hid(step + 4, k // 2)
+                    transpose_hid(step + 5, k // 2)
             transpose_v(step + 5)

@@ -148,8 +148,7 @@ def tile_akgcn_pb_t_kernel(tc, x, hid, adj, lam_raw, theta_words, theta_scales, 
             if not 0 <= part < PARTS:
                 return
             vT_grouped[part] = work.tile([P, P, PACK], BF16, name="vT_grouped", align_bytes=64)
-            copy = nc.scalar.copy if part % 2 == 0 else nc.vector.tensor_copy
-            copy(out=vT_grouped[part][:], in_=vT_ps[part][:].rearrange("q t p -> q p t"))
+            nc.vector.tensor_copy(out=vT_grouped[part][:], in_=vT_ps[part][:].rearrange("q t p -> q p t"))
 
         def quantise_v(part):
             if not 0 <= part < PARTS:
@@ -207,7 +206,8 @@ def tile_akgcn_pb_t_kernel(tc, x, hid, adj, lam_raw, theta_words, theta_scales, 
                     start=True,
                     stop=True,
                 )
-            nc.scalar.copy(out=h_grouped[u][:, cols(cb), :], in_=h_ps[:].rearrange("p j c -> p c j"))
+            copy = nc.vector.tensor_copy if u // T == B - 1 and cb == C // P - 1 else nc.scalar.copy
+            copy(out=h_grouped[u][:, cols(cb), :], in_=h_ps[:].rearrange("p j c -> p c j"))
 
         def quantise_h(u):
             if not 0 <= u < UNITS:

@@ -140,15 +140,18 @@ def tile_akgcn_pb_t_kernel(tc, x, hid, adj, lam_raw, theta_words, theta_scales, 
         def transpose_v(part):
             if not 0 <= part < PARTS:
                 return
-            vT_ps[part] = psum_vT.tile([P, PACK, P], BF16, name="vT_ps")
-            for t in range(PACK):
-                nc.tensor.transpose(vT_ps[part][:, t, :], v_rows[part][:, t:N:PACK], ident_bf[:])
+            v_words = v_rows[part][:].bitcast(F32)
+            vT_ps[part] = psum_vT.tile([P, 2, P], F32, name="vT_ps")
+            for pair in range(2):
+                nc.tensor.transpose(vT_ps[part][:, pair, :], v_words[:, pair : N // 2 : 2], ident_f32[:])
 
         def group_v(part):
             if not 0 <= part < PARTS:
                 return
             vT_grouped[part] = work.tile([P, P, PACK], BF16, name="vT_grouped", align_bytes=64)
-            nc.vector.tensor_copy(out=vT_grouped[part][:], in_=vT_ps[part][:].rearrange("q t p -> q p t"))
+            nc.vector.tensor_copy(
+                out=vT_grouped[part][:].bitcast(F32), in_=vT_ps[part][:].rearrange("q pair p -> q p pair")
+            )
 
         def quantise_v(part):
             if not 0 <= part < PARTS:

@@ -87,10 +87,12 @@ def tile_akgcn_pb_t_kernel(tc, x, hid, adj, lam_raw, theta_words, theta_scales, 
         ident_bf = consts.tile([P, P], BF16)
         make_identity(nc, ident_bf[:])
 
-        w = consts.tile([P, 1], F32)
-        nc.vector.tensor_scalar_max(out=w[:], in0=lam_bf[:], scalar1=0.0)
+        load_hid(1)
+
         w_diag = consts.tile([P, PACK, N], BF16)
         nc.vector.memset(w_diag[:], 0.0)
+        w = consts.tile([P, 1], F32)
+        nc.vector.tensor_scalar_max(out=w[:], in0=lam_bf[:], scalar1=0.0)
         for i in range(PACK):
             nc.vector.tensor_scalar(
                 out=w_diag[:, i, :].rearrange("p (q t) -> p q t", t=PACK)[:, :, i],
@@ -215,8 +217,8 @@ def tile_akgcn_pb_t_kernel(tc, x, hid, adj, lam_raw, theta_words, theta_scales, 
         def quantise_h(u):
             if not 0 <= u < UNITS:
                 return
-            h_codes[u] = work.tile([P, C], U32, name="h_codes", align_bytes=64)
-            h_plane[u] = work.tile([P, C], U8, name="h_plane", align_bytes=64)
+            h_codes[u] = work.tile([P, C], U32, name="h_codes", align_bytes=64, bufs=4)
+            h_plane[u] = work.tile([P, C], U8, name="h_plane", align_bytes=64, bufs=4)
             nc.vector.quantize_mx(
                 out=h_codes[u][:].bitcast(FP8X4),
                 scales=h_plane[u][:],
@@ -249,7 +251,7 @@ def tile_akgcn_pb_t_kernel(tc, x, hid, adj, lam_raw, theta_words, theta_scales, 
         def finish(u):
             if not 0 <= u < UNITS:
                 return
-            groups = 1 if u == UNITS - 1 else PACK
+            groups = 1 if u == UNITS - 1 else 2
             for first in range(0, PACK, groups):
                 piece = slice(first, first + groups)
                 flat = out_sb[u][:, piece, :].rearrange("p i c -> p (i c)")
@@ -263,24 +265,24 @@ def tile_akgcn_pb_t_kernel(tc, x, hid, adj, lam_raw, theta_words, theta_scales, 
                 )
                 nc.sync.dma_start(out=out_units[u][:, piece, :], in_=out_sb[u][:, piece, :])
 
-        for step in range(-6, UNITS + 1):
-            load_adj(step + 8)
+        for step in range(-5, UNITS + 1):
+            load_adj(step + 7)
             load_hid(step + 7)
             load_x(step + 3)
 
-            finish(step - 1)
-            sum_v_rows(step + 6)
             quantise_hid(step + 4)
-            invert_v_sums(step + 6)
+            sum_v_rows(step + 5)
+            finish(step - 1)
             group_v(step + 4)
-            scale_v_rows(step + 6)
-            quantise_h(step + 1)
-            relu_x(step)
+            invert_v_sums(step + 5)
+            quantise_h(step + 2)
+            scale_v_rows(step + 5)
             quantise_v(step + 4)
+            relu_x(step + 1)
 
             for k in range(PACK):
-                first_matmul(step + 2, k)
                 second_matmul(step, k)
-                if k % 2 == 1:
-                    transpose_hid(step + 5, k // 2)
+                first_matmul(step + 3, k)
+                if k < 2:
+                    transpose_hid(step + 5, k)
             transpose_v(step + 5)

@@ -56,12 +56,12 @@ def tile_akgcn_pb_t_kernel(tc, x, hid, adj, lam_raw, theta_words, theta_scales, 
 
         def load_hid(u):
             if 0 <= u < UNITS and u not in hid_sb:
-                hid_sb[u] = loads.tile([P, PACK, C], BF16, name="hid_sb")
+                hid_sb[u] = loads.tile([P, PACK, C], BF16, name="hid_sb", bufs=6)
                 nc.sync.dma_start(out=hid_sb[u][:], in_=hid_units[u])
 
         def load_x(u):
             if 0 <= u < UNITS:
-                x_sb[u] = loads.tile([P, PACK, C], BF16, name="x_sb", bufs=5)
+                x_sb[u] = loads.tile([P, PACK, C], BF16, name="x_sb", bufs=8)
                 nc.sync.dma_start(out=x_sb[u][:], in_=x_units[u])
 
         load_hid(0)
@@ -130,7 +130,7 @@ def tile_akgcn_pb_t_kernel(tc, x, hid, adj, lam_raw, theta_words, theta_scales, 
         def scale_v_rows(part):
             if not 0 <= part < PARTS:
                 return
-            v_rows[part] = work.tile([P, N], BF16, name="v_rows")
+            v_rows[part] = work.tile([P, N], BF16, name="v_rows", bufs=3)
             nc.vector.tensor_scalar(
                 out=v_rows[part][:],
                 in0=with_diag[part][:],
@@ -229,7 +229,7 @@ def tile_akgcn_pb_t_kernel(tc, x, hid, adj, lam_raw, theta_words, theta_scales, 
             if not 0 <= u < UNITS:
                 return
             if i == 0:
-                out_sb[u] = loads.tile([P, PACK, C], F32, name="out_sb")
+                out_sb[u] = loads.tile([P, PACK, C], F32, name="out_sb", bufs=6)
             part = (u // T) * PACK + i
             g_ps = psum_g.tile([P, C], F32, name="g_ps")
             nc.tensor.matmul_mx(
@@ -265,24 +265,33 @@ def tile_akgcn_pb_t_kernel(tc, x, hid, adj, lam_raw, theta_words, theta_scales, 
                 )
                 nc.sync.dma_start(out=out_units[u][:, piece, :], in_=out_sb[u][:, piece, :])
 
-        for step in range(-5, UNITS + 1):
-            load_adj(step + 7)
-            load_hid(step + 7)
-            load_x(step + 3)
+        transpose_hid(0, 0)
+        transpose_hid(0, 1)
+        sum_v_rows(0)
+        quantise_hid(0)
+        for k in range(PACK):
+            first_matmul(0, k)
+        for step in range(-6, UNITS + 1):
+            load_adj(step + 8)
+            load_hid(step + 8)
+            load_x(step + 4)
 
-            quantise_hid(step + 4)
-            sum_v_rows(step + 5)
+            if step > -6:
+                sum_v_rows(step + 6)
             finish(step - 1)
+            if step > -4:
+                quantise_hid(step + 4)
+            invert_v_sums(step + 6)
             group_v(step + 4)
-            invert_v_sums(step + 5)
             quantise_h(step + 2)
-            scale_v_rows(step + 5)
+            scale_v_rows(step + 6)
             quantise_v(step + 4)
             relu_x(step + 1)
 
             for k in range(PACK):
                 second_matmul(step, k)
-                first_matmul(step + 3, k)
-                if k < 2:
-                    transpose_hid(step + 5, k)
+                if step > -3:
+                    first_matmul(step + 3, k)
+                if k in (1, 3) and step > -5:
+                    transpose_hid(step + 5, int(k == 3))
             transpose_v(step + 5)

@@ -36,10 +36,8 @@ def tile_akgcn_pb_t_kernel(tc, x, hid, adj, lam_raw, theta_words, theta_scales, 
         loads = stack.enter_context(tc.tile_pool(name="loads", bufs=4))
         work = stack.enter_context(tc.tile_pool(name="work", bufs=2))
         small = stack.enter_context(tc.tile_pool(name="small", bufs=4))
-        psum_hidT = stack.enter_context(tc.psum_pool(name="psum_hidT", bufs=2))
-        psum_vT = stack.enter_context(tc.psum_pool(name="psum_vT", bufs=1))
-        psum_h = stack.enter_context(tc.psum_pool(name="psum_h", bufs=3))
-        psum_g = stack.enter_context(tc.psum_pool(name="psum_g", bufs=2))
+        psum_vT = stack.enter_context(tc.psum_pool(name="psum_vT", bufs=2))
+        psum = stack.enter_context(tc.psum_pool(name="psum", bufs=6))
 
         stack.enter_context(tc.manual_schedule())
 
@@ -171,7 +169,7 @@ def tile_akgcn_pb_t_kernel(tc, x, hid, adj, lam_raw, theta_words, theta_scales, 
                 hidT_grouped[u] = work.tile([P, PACK, P, PACK], BF16, name="hidT_grouped", align_bytes=64)
             hid_words = hid_sb[u][:].bitcast(F32)
             grouped_words = hidT_grouped[u][:].bitcast(F32)
-            hidT_ps = psum_hidT.tile([P, 2, 2, P], F32, name="hidT_ps")
+            hidT_ps = psum.tile([P, 2, 2, P], F32, name="bank")
             for jj in range(2):
                 for pair in range(2):
                     nc.tensor.transpose(
@@ -200,7 +198,7 @@ def tile_akgcn_pb_t_kernel(tc, x, hid, adj, lam_raw, theta_words, theta_scales, 
                 return
             if cb == 0:
                 h_grouped[u] = work.tile([P, C, PACK], BF16, name="h_grouped", align_bytes=64)
-            h_ps = psum_h.tile([P, PACK, P], F32, name="h_ps")
+            h_ps = psum.tile([P, PACK, P], F32, name="bank")
             for j in range(PACK):
                 nc.tensor.matmul_mx(
                     out=h_ps[:, j, :],
@@ -231,7 +229,7 @@ def tile_akgcn_pb_t_kernel(tc, x, hid, adj, lam_raw, theta_words, theta_scales, 
             if i == 0:
                 out_sb[u] = loads.tile([P, PACK, C], F32, name="out_sb", bufs=6)
             part = (u // T) * PACK + i
-            g_ps = psum_g.tile([P, C], F32, name="g_ps")
+            g_ps = psum.tile([P, C], F32, name="bank")
             nc.tensor.matmul_mx(
                 out=g_ps[:],
                 lhsT=vT_codes[:, part, :].bitcast(FP8X4),
@@ -274,19 +272,19 @@ def tile_akgcn_pb_t_kernel(tc, x, hid, adj, lam_raw, theta_words, theta_scales, 
         for step in range(-6, UNITS + 1):
             load_adj(step + 8)
             load_hid(step + 8)
-            load_x(step + 4)
+            load_x(step + 6)
 
             if step > -6:
                 sum_v_rows(step + 6)
             finish(step - 1)
+            group_v(step + 4)
+            invert_v_sums(step + 6)
             if step > -4:
                 quantise_hid(step + 4)
-            invert_v_sums(step + 6)
-            group_v(step + 4)
             quantise_h(step + 2)
-            scale_v_rows(step + 6)
             quantise_v(step + 4)
-            relu_x(step + 1)
+            scale_v_rows(step + 6)
+            relu_x(step + 3)
 
             for k in range(PACK):
                 second_matmul(step, k)

@@ -43,8 +43,7 @@ def tile_akgcn_pb_t_kernel(tc, x, hid, adj, lam_raw, theta_words, theta_scales, 
 
         adj_sb, hid_sb, x_sb, out_sb = {}, {}, {}, {}
         with_diag, row_sum, inv_sum, v_rows, vT_ps, vT_grouped = {}, {}, {}, {}, {}, {}
-        hidT_grouped, hid_codes, hid_plane = {}, {}, {}
-        h_grouped, h_codes, h_plane = {}, {}, {}
+        grouped, codes, plane = {}, {}, {}
 
         def load_adj(part):
             b = part // PACK
@@ -162,13 +161,30 @@ def tile_akgcn_pb_t_kernel(tc, x, hid, adj, lam_raw, theta_words, theta_scales, 
                 in_=vT_grouped[part][:].rearrange("q p t -> q (p t)"),
             )
 
+        def grouped_tile(step):
+            if step not in grouped:
+                grouped[step] = work.tile([P, 2, N * PACK], BF16, name="grouped", align_bytes=64, bufs=4)
+            return grouped[step]
+
+        def quantise(step):
+            if not -4 <= step < UNITS - 2:
+                return
+            slots = slice(0 if step + 4 < UNITS else 1, 2 if step + 2 >= 0 else 1)
+            codes[step] = work.tile([P, 2, N], U32, name="codes", align_bytes=64, bufs=4)
+            plane[step] = work.tile([P, 2, N], U8, name="plane", align_bytes=64, bufs=4)
+            nc.vector.quantize_mx(
+                out=codes[step][:, slots, :].rearrange("q s n -> q (s n)").bitcast(FP8X4),
+                scales=plane[step][:, slots, :].rearrange("q s n -> q (s n)"),
+                in_=grouped[step][:, slots, :].rearrange("q s n -> q (s n)"),
+            )
+
         def transpose_hid(u, half):
             if not 0 <= u < UNITS:
                 return
-            if half == 0:
-                hidT_grouped[u] = work.tile([P, PACK, P, PACK], BF16, name="hidT_grouped", align_bytes=64)
             hid_words = hid_sb[u][:].bitcast(F32)
-            grouped_words = hidT_grouped[u][:].bitcast(F32)
+            grouped_words = grouped_tile(u - 4)[:, 0, :].bitcast(F32).rearrange(
+                "q (j p pair) -> q j p pair", j=PACK, pair=2
+            )
             hidT_ps = psum.tile([P, 2, 2, P], F32, name="bank")
             for jj in range(2):
                 for pair in range(2):
@@ -182,46 +198,23 @@ def tile_akgcn_pb_t_kernel(tc, x, hid, adj, lam_raw, theta_words, theta_scales, 
                 in_=hidT_ps[:].rearrange("q jj pair p -> q jj p pair"),
             )
 
-        def quantise_hid(u):
-            if not 0 <= u < UNITS:
-                return
-            hid_codes[u] = work.tile([P, N], U32, name="hid_codes", align_bytes=64, bufs=3)
-            hid_plane[u] = work.tile([P, N], U8, name="hid_plane", align_bytes=64, bufs=3)
-            nc.vector.quantize_mx(
-                out=hid_codes[u][:].bitcast(FP8X4),
-                scales=hid_plane[u][:],
-                in_=hidT_grouped[u][:].rearrange("q j p t -> q (j p t)"),
-            )
-
         def first_matmul(u, cb):
             if not 0 <= u < UNITS:
                 return
-            if cb == 0:
-                h_grouped[u] = work.tile([P, C, PACK], BF16, name="h_grouped", align_bytes=64)
+            h_grouped = grouped_tile(u - 2)[:, 1, :].rearrange("p (c j) -> p c j", j=PACK)
             h_ps = psum.tile([P, PACK, P], F32, name="bank")
             for j in range(PACK):
                 nc.tensor.matmul_mx(
                     out=h_ps[:, j, :],
-                    lhsT=hid_codes[u][:, cols(j)].bitcast(FP8X4),
-                    lhsT_scale=hid_plane[u][:, cols(j)],
+                    lhsT=codes[u - 4][:, 0, cols(j)].bitcast(FP8X4),
+                    lhsT_scale=plane[u - 4][:, 0, cols(j)],
                     rhs=theta_codes[:, cols(cb)].bitcast(FP8X4),
                     rhs_scale=theta_plane[:, cols(cb)],
                     start=True,
                     stop=True,
                 )
-            copy = nc.vector.tensor_copy if u // T == B - 1 and cb == C // P - 1 else nc.scalar.copy
-            copy(out=h_grouped[u][:, cols(cb), :], in_=h_ps[:].rearrange("p j c -> p c j"))
-
-        def quantise_h(u):
-            if not 0 <= u < UNITS:
-                return
-            h_codes[u] = work.tile([P, C], U32, name="h_codes", align_bytes=64, bufs=4)
-            h_plane[u] = work.tile([P, C], U8, name="h_plane", align_bytes=64, bufs=4)
-            nc.vector.quantize_mx(
-                out=h_codes[u][:].bitcast(FP8X4),
-                scales=h_plane[u][:],
-                in_=h_grouped[u][:].rearrange("p c j -> p (c j)"),
-            )
+            copy = nc.vector.tensor_copy if UNITS - T <= u < UNITS - 1 and cb == C // P - 1 else nc.scalar.copy
+            copy(out=h_grouped[:, cols(cb), :], in_=h_ps[:].rearrange("p j c -> p c j"))
 
         def second_matmul(u, i):
             if not 0 <= u < UNITS:
@@ -234,8 +227,8 @@ def tile_akgcn_pb_t_kernel(tc, x, hid, adj, lam_raw, theta_words, theta_scales, 
                 out=g_ps[:],
                 lhsT=vT_codes[:, part, :].bitcast(FP8X4),
                 lhsT_scale=vT_plane[:, part, :],
-                rhs=h_codes[u][:].bitcast(FP8X4),
-                rhs_scale=h_plane[u][:],
+                rhs=codes[u - 2][:, 1, :].bitcast(FP8X4),
+                rhs_scale=plane[u - 2][:, 1, :],
                 start=True,
                 stop=True,
             )
@@ -266,7 +259,7 @@ def tile_akgcn_pb_t_kernel(tc, x, hid, adj, lam_raw, theta_words, theta_scales, 
         transpose_hid(0, 0)
         transpose_hid(0, 1)
         sum_v_rows(0)
-        quantise_hid(0)
+        quantise(-4)
         for k in range(PACK):
             first_matmul(0, k)
         for step in range(-6, UNITS + 1):
@@ -280,8 +273,7 @@ def tile_akgcn_pb_t_kernel(tc, x, hid, adj, lam_raw, theta_words, theta_scales, 
             group_v(step + 4)
             invert_v_sums(step + 6)
             if step > -4:
-                quantise_hid(step + 4)
-            quantise_h(step + 2)
+                quantise(step)
             quantise_v(step + 4)
             scale_v_rows(step + 6)
             relu_x(step + 3)

@@ -54,16 +54,19 @@ def tile_akgcn_pb_t_kernel(tc, x, hid, adj, lam_raw, theta_words, theta_scales, 
         def load_hid(u):
             if 0 <= u < UNITS and u not in hid_sb:
                 hid_sb[u] = loads.tile([P, PACK, C], BF16, name="hid_sb", bufs=6)
-                nc.sync.dma_start(out=hid_sb[u][:], in_=hid_units[u])
+                pieces = 2 if u == 0 else 1
+                for piece in range(pieces):
+                    rows = slice(piece * PACK // pieces, (piece + 1) * PACK // pieces)
+                    nc.sync.dma_start(out=hid_sb[u][:, rows, :], in_=hid_units[u][:, rows, :])
 
         def load_x(u):
             if 0 <= u < UNITS:
                 x_sb[u] = loads.tile([P, PACK, C], BF16, name="x_sb", bufs=8)
                 nc.sync.dma_start(out=x_sb[u][:], in_=x_units[u])
 
-        load_hid(0)
         lam_bf = consts.tile([P, 1], BF16)
         nc.sync.dma_start(out=lam_bf[:], in_=lam_raw.partition_broadcast(P))
+        load_hid(0)
         load_adj(0)
 
         theta_plane = consts.tile([P, C], U8, align_bytes=64)
@@ -73,6 +76,15 @@ def tile_akgcn_pb_t_kernel(tc, x, hid, adj, lam_raw, theta_words, theta_scales, 
                 out=theta_plane[32 * quadrant : 32 * quadrant + 4, :].bitcast(I32),
                 in_=theta_scales[0, 4 * quadrant : 4 * quadrant + 4, :].bitcast(I32),
             )
+        zeros = consts.tile([P, C], BF16)
+        nc.vector.memset(zeros[:], 0.0)
+
+        def warm_up(passes):
+            for again in range(passes):
+                bank = psum.tile([P, C], F32, name="bank")
+                nc.tensor.matmul(bank[:], lhsT=zeros[:, :P], rhs=zeros[:], start=True, stop=True)
+
+        warm_up(5)
         theta_codes = consts.tile([P, C], U32, align_bytes=64)
         nc.sync.dma_start(
             out=theta_codes[:].bitcast(I32),
@@ -81,23 +93,23 @@ def tile_akgcn_pb_t_kernel(tc, x, hid, adj, lam_raw, theta_words, theta_scales, 
 
         ident_f32 = consts.tile([P, P], F32)
         make_identity(nc, ident_f32[:])
-        ident_bf = consts.tile([P, P], BF16)
-        make_identity(nc, ident_bf[:])
+        diagonal = consts.tile([P, PACK, N], BF16)
+        nc.vector.memset(diagonal[:], 0.0)
+        for i in range(PACK):
+            nc.gpsimd.affine_select(
+                out=diagonal[:, i, :],
+                in_=diagonal[:, i, :],
+                pattern=[[-1, N]],
+                compare_op=ALU.not_equal,
+                fill=1.0,
+                base=i,
+                channel_multiplier=PACK,
+            )
 
         load_hid(1)
 
-        w_diag = consts.tile([P, PACK, N], BF16)
-        nc.vector.memset(w_diag[:], 0.0)
         w = consts.tile([P, 1], F32)
         nc.vector.tensor_scalar_max(out=w[:], in0=lam_bf[:], scalar1=0.0)
-        for i in range(PACK):
-            nc.vector.tensor_scalar(
-                out=w_diag[:, i, :].rearrange("p (q t) -> p q t", t=PACK)[:, :, i],
-                in0=ident_bf[:],
-                scalar1=w[:, 0:1],
-                scalar2=None,
-                op0=ALU.mult,
-            )
 
         vT_codes = consts.tile([P, PARTS, P], U32, align_bytes=64)
         vT_plane = consts.tile([P, PARTS, P], U8, align_bytes=64)
@@ -110,9 +122,9 @@ def tile_akgcn_pb_t_kernel(tc, x, hid, adj, lam_raw, theta_words, theta_scales, 
             row_sum[part] = small.tile([P, 1], F32, name="row_sum")
             nc.vector.scalar_tensor_tensor(
                 out=with_diag[part][:],
-                in0=adj_sb[b][:, i, :],
-                scalar=1.0,
-                in1=w_diag[:, i, :],
+                in0=diagonal[:, i, :],
+                scalar=w[:, 0:1],
+                in1=adj_sb[b][:, i, :],
                 op0=ALU.mult,
                 op1=ALU.add,
                 accum_out=row_sum[part][:],
@@ -242,7 +254,7 @@ def tile_akgcn_pb_t_kernel(tc, x, hid, adj, lam_raw, theta_words, theta_scales, 
         def finish(u):
             if not 0 <= u < UNITS:
                 return
-            groups = 1 if u == UNITS - 1 else 2
+            groups = 1 if u // T == B - 1 else 2
             for first in range(0, PACK, groups):
                 piece = slice(first, first + groups)
                 flat = out_sb[u][:, piece, :].rearrange("p i c -> p (i c)")
@@ -258,6 +270,7 @@ def tile_akgcn_pb_t_kernel(tc, x, hid, adj, lam_raw, theta_words, theta_scales, 
 
         transpose_hid(0, 0)
         transpose_hid(0, 1)
+        warm_up(2)
         sum_v_rows(0)
         quantise(-4)
         for k in range(PACK):

from contextlib import ExitStack

import concourse.mybir as mybir
from concourse.masks import make_identity

F32 = mybir.dt.float32
BF16 = mybir.dt.bfloat16
I32 = mybir.dt.int32
U32 = mybir.dt.uint32
U8 = mybir.dt.uint8
FP8X4 = mybir.dt.float8_e4m3fn_x4
ALU = mybir.AluOpType
ACT = mybir.ActivationFunctionType

P = 128
PACK = 4
B, T, N, C = 4, 4, 512, 512
UNITS = B * T
PARTS = B * PACK
FLOPS = 2 * B * T * N * C * C + 2 * B * T * N * N * C


def cols(k):
    return slice(k * P, (k + 1) * P)


def tile_akgcn_pb_t_kernel(tc, x, hid, adj, lam_raw, theta_words, theta_scales, out):
    nc = tc.nc
    hid_units = hid.rearrange("b t (p j) c -> (b t) p j c", j=PACK)
    x_units = x.rearrange("b t (p i) c -> (b t) p i c", i=PACK)
    out_units = out.rearrange("b t (p i) c -> (b t) p i c", i=PACK)
    adj_rows = adj.rearrange("b (p i) m -> b p i m", i=PACK)

    with ExitStack() as stack:
        consts = stack.enter_context(tc.tile_pool(name="consts", bufs=1))
        loads = stack.enter_context(tc.tile_pool(name="loads", bufs=4))
        work = stack.enter_context(tc.tile_pool(name="work", bufs=2))
        small = stack.enter_context(tc.tile_pool(name="small", bufs=4))
        psum_vT = stack.enter_context(tc.psum_pool(name="psum_vT", bufs=2))
        psum = stack.enter_context(tc.psum_pool(name="psum", bufs=6))

        stack.enter_context(tc.manual_schedule())

        adj_sb, hid_sb, x_sb, out_sb = {}, {}, {}, {}
        with_diag, row_sum, inv_sum, v_rows, vT_ps, vT_grouped = {}, {}, {}, {}, {}, {}
        grouped, codes, plane = {}, {}, {}

        def load_adj(part):
            b = part // PACK
            if 0 <= part < PARTS and b not in adj_sb:
                adj_sb[b] = loads.tile([P, PACK, N], BF16, name="adj_sb", bufs=2)
                nc.sync.dma_start(out=adj_sb[b][:], in_=adj_rows[b])

        def load_hid(u):
            if 0 <= u < UNITS and u not in hid_sb:
                hid_sb[u] = loads.tile([P, PACK, C], BF16, name="hid_sb", bufs=6)
                pieces = 2 if u == 0 else 1
                for piece in range(pieces):
                    rows = slice(piece * PACK // pieces, (piece + 1) * PACK // pieces)
                    nc.sync.dma_start(out=hid_sb[u][:, rows, :], in_=hid_units[u][:, rows, :])

        def load_x(u):
            if 0 <= u < UNITS:
                x_sb[u] = loads.tile([P, PACK, C], BF16, name="x_sb", bufs=8)
                nc.sync.dma_start(out=x_sb[u][:], in_=x_units[u])

        lam_bf = consts.tile([P, 1], BF16)
        nc.sync.dma_start(out=lam_bf[:], in_=lam_raw.partition_broadcast(P))
        load_hid(0)
        load_adj(0)

        theta_plane = consts.tile([P, C], U8, align_bytes=64)
        nc.vector.memset(theta_plane[:].bitcast(I32), 0)
        for quadrant in range(4):
            nc.sync.dma_start(
                out=theta_plane[32 * quadrant : 32 * quadrant + 4, :].bitcast(I32),
                in_=theta_scales[0, 4 * quadrant : 4 * quadrant + 4, :].bitcast(I32),
            )
        zeros = consts.tile([P, C], BF16)
        nc.vector.memset(zeros[:], 0.0)

        def warm_up(passes):
            for again in range(passes):
                bank = psum.tile([P, C], F32, name="bank")
                nc.tensor.matmul(bank[:], lhsT=zeros[:, :P], rhs=zeros[:], start=True, stop=True)

        warm_up(5)
        theta_codes = consts.tile([P, C], U32, align_bytes=64)
        nc.sync.dma_start(
            out=theta_codes[:].bitcast(I32),
            in_=theta_words[0].rearrange("p n t -> p (n t)").bitcast(I32),
        )

        ident_f32 = consts.tile([P, P], F32)
        make_identity(nc, ident_f32[:])
        diagonal = consts.tile([P, PACK, N], BF16)
        nc.vector.memset(diagonal[:], 0.0)
        for i in range(PACK):
            nc.gpsimd.affine_select(
                out=diagonal[:, i, :],
                in_=diagonal[:, i, :],
                pattern=[[-1, N]],
                compare_op=ALU.not_equal,
                fill=1.0,
                base=i,
                channel_multiplier=PACK,
            )

        load_hid(1)

        w = consts.tile([P, 1], F32)
        nc.vector.tensor_scalar_max(out=w[:], in0=lam_bf[:], scalar1=0.0)

        vT_codes = consts.tile([P, PARTS, P], U32, align_bytes=64)
        vT_plane = consts.tile([P, PARTS, P], U8, align_bytes=64)

        def sum_v_rows(part):
            if not 0 <= part < PARTS:
                return
            b, i = divmod(part, PACK)
            with_diag[part] = work.tile([P, N], F32, name="with_diag")
            row_sum[part] = small.tile([P, 1], F32, name="row_sum")
            nc.vector.scalar_tensor_tensor(
                out=with_diag[part][:],
                in0=diagonal[:, i, :],
                scalar=w[:, 0:1],
                in1=adj_sb[b][:, i, :],
                op0=ALU.mult,
                op1=ALU.add,
                accum_out=row_sum[part][:],
            )

        def invert_v_sums(part):
            if not 0 <= part < PARTS:
                return
            inv_sum[part] = small.tile([P, 1], F32, name="inv_sum")
            nc.vector.reciprocal(out=inv_sum[part][:], in_=row_sum[part][:])

        def scale_v_rows(part):
            if not 0 <= part < PARTS:
                return
            v_rows[part] = work.tile([P, N], BF16, name="v_rows", bufs=3)
            nc.vector.tensor_scalar(
                out=v_rows[part][:],
                in0=with_diag[part][:],
                scalar1=inv_sum[part][:, 0:1],
                scalar2=None,
                op0=ALU.mult,
            )

        def transpose_v(part):
            if not 0 <= part < PARTS:
                return
            v_words = v_rows[part][:].bitcast(F32)
            vT_ps[part] = psum_vT.tile([P, 2, P], F32, name="vT_ps")
            for pair in range(2):
                nc.tensor.transpose(vT_ps[part][:, pair, :], v_words[:, pair : N // 2 : 2], ident_f32[:])

        def group_v(part):
            if not 0 <= part < PARTS:
                return
            vT_grouped[part] = work.tile([P, P, PACK], BF16, name="vT_grouped", align_bytes=64)
            nc.vector.tensor_copy(
                out=vT_grouped[part][:].bitcast(F32), in_=vT_ps[part][:].rearrange("q pair p -> q p pair")
            )

        def quantise_v(part):
            if not 0 <= part < PARTS:
                return
            nc.vector.quantize_mx(
                out=vT_codes[:, part, :].bitcast(FP8X4),
                scales=vT_plane[:, part, :],
                in_=vT_grouped[part][:].rearrange("q p t -> q (p t)"),
            )

        def grouped_tile(step):
            if step not in grouped:
                grouped[step] = work.tile([P, 2, N * PACK], BF16, name="grouped", align_bytes=64, bufs=4)
            return grouped[step]

        def quantise(step):
            if not -4 <= step < UNITS - 2:
                return
            slots = slice(0 if step + 4 < UNITS else 1, 2 if step + 2 >= 0 else 1)
            codes[step] = work.tile([P, 2, N], U32, name="codes", align_bytes=64, bufs=4)
            plane[step] = work.tile([P, 2, N], U8, name="plane", align_bytes=64, bufs=4)
            nc.vector.quantize_mx(
                out=codes[step][:, slots, :].rearrange("q s n -> q (s n)").bitcast(FP8X4),
                scales=plane[step][:, slots, :].rearrange("q s n -> q (s n)"),
                in_=grouped[step][:, slots, :].rearrange("q s n -> q (s n)"),
            )

        def transpose_hid(u, half):
            if not 0 <= u < UNITS:
                return
            hid_words = hid_sb[u][:].bitcast(F32)
            grouped_words = grouped_tile(u - 4)[:, 0, :].bitcast(F32).rearrange(
                "q (j p pair) -> q j p pair", j=PACK, pair=2
            )
            hidT_ps = psum.tile([P, 2, 2, P], F32, name="bank")
            for jj in range(2):
                for pair in range(2):
                    nc.tensor.transpose(
                        hidT_ps[:, jj, pair, :],
                        hid_words[:, 2 * half + jj, pair : C // 2 : 2],
                        ident_f32[:],
                    )
            nc.scalar.copy(
                out=grouped_words[:, 2 * half : 2 * half + 2, :, :],
                in_=hidT_ps[:].rearrange("q jj pair p -> q jj p pair"),
            )

        def first_matmul(u, cb):
            if not 0 <= u < UNITS:
                return
            h_grouped = grouped_tile(u - 2)[:, 1, :].rearrange("p (c j) -> p c j", j=PACK)
            h_ps = psum.tile([P, PACK, P], F32, name="bank")
            for j in range(PACK):
                nc.tensor.matmul_mx(
                    out=h_ps[:, j, :],
                    lhsT=codes[u - 4][:, 0, cols(j)].bitcast(FP8X4),
                    lhsT_scale=plane[u - 4][:, 0, cols(j)],
                    rhs=theta_codes[:, cols(cb)].bitcast(FP8X4),
                    rhs_scale=theta_plane[:, cols(cb)],
                    start=True,
                    stop=True,
                )
            copy = nc.vector.tensor_copy if UNITS - T <= u < UNITS - 1 and cb == C // P - 1 else nc.scalar.copy
            copy(out=h_grouped[:, cols(cb), :], in_=h_ps[:].rearrange("p j c -> p c j"))

        def second_matmul(u, i):
            if not 0 <= u < UNITS:
                return
            if i == 0:
                out_sb[u] = loads.tile([P, PACK, C], F32, name="out_sb", bufs=6)
            part = (u // T) * PACK + i
            g_ps = psum.tile([P, C], F32, name="bank")
            nc.tensor.matmul_mx(
                out=g_ps[:],
                lhsT=vT_codes[:, part, :].bitcast(FP8X4),
                lhsT_scale=vT_plane[:, part, :],
                rhs=codes[u - 2][:, 1, :].bitcast(FP8X4),
                rhs_scale=plane[u - 2][:, 1, :],
                start=True,
                stop=True,
            )
            nc.scalar.activation(out=out_sb[u][:, i, :], in_=g_ps[:], func=ACT.Sigmoid)

        def relu_x(u):
            if not 0 <= u < UNITS:
                return
            nc.vector.tensor_scalar_max(out=x_sb[u][:], in0=x_sb[u][:], scalar1=0.0)

        def finish(u):
            if not 0 <= u < UNITS:
                return
            groups = 1 if u // T == B - 1 else 2
            for first in range(0, PACK, groups):
                piece = slice(first, first + groups)
                flat = out_sb[u][:, piece, :].rearrange("p i c -> p (i c)")
                nc.vector.scalar_tensor_tensor(
                    out=flat,
                    in0=flat,
                    scalar=0.5,
                    in1=x_sb[u][:, piece, :].rearrange("p i c -> p (i c)"),
                    op0=ALU.max,
                    op1=ALU.add,
                )
                nc.sync.dma_start(out=out_units[u][:, piece, :], in_=out_sb[u][:, piece, :])

        transpose_hid(0, 0)
        transpose_hid(0, 1)
        warm_up(2)
        sum_v_rows(0)
        quantise(-4)
        for k in range(PACK):
            first_matmul(0, k)
        for step in range(-6, UNITS + 1):
            load_adj(step + 8)
            load_hid(step + 8)
            load_x(step + 6)

            if step > -6:
                sum_v_rows(step + 6)
            finish(step - 1)
            group_v(step + 4)
            invert_v_sums(step + 6)
            if step > -4:
                quantise(step)
            quantise_v(step + 4)
            scale_v_rows(step + 6)
            relu_x(step + 3)

            for k in range(PACK):
                second_matmul(step, k)
                if step > -3:
                    first_matmul(step + 3, k)
                if k in (1, 3) and step > -5:
                    transpose_hid(step + 5, int(k == 3))
            transpose_v(step + 5)
